import numpy as np
import ml_dtypes


def mxq(x, axis, fmt="e4m3"):
    dtype, down = {"e4m3": (ml_dtypes.float8_e4m3fn, 7), "e5m2": (ml_dtypes.float8_e5m2, 14)}[fmt]
    v = np.moveaxis(np.asarray(x, np.float32).astype(ml_dtypes.bfloat16).astype(np.float64), axis, -1)
    blocks = v.reshape(v.shape[:-1] + (-1, 32))
    amax = np.abs(blocks).max(-1, keepdims=True)
    byte = np.maximum(np.where(amax > 0, np.frexp(amax)[1] - 1 + 127, 0) - down, 1)
    scale = np.exp2(byte - 127.0)
    codes = (blocks / scale).astype(np.float32).astype(dtype).astype(np.float64)
    return np.moveaxis((codes * scale).reshape(v.shape), -1, axis)


WIDE = False


def mx_kscale(k):
    if not WIDE:
        return np.ones(k)
    levels = np.array([10, -10, 5, -5, 0])
    a = np.random.permutation(np.resize(levels, k // 512 * 4)).reshape(k // 512, 4)
    idx = np.arange(k)
    return np.exp2(a[idx // 512, idx % 128 // 32])


BF16 = ml_dtypes.bfloat16


def bf(x):
    return np.asarray(x, np.float32).astype(BF16)


def f64(x):
    return np.asarray(x).astype(np.float64)


B, T, C, H, S, L, QB = 4, 768, 512, 4, 256, 1024, 512
HD = C // H
N = S + T
THETA = 10000.0


def rope_cos_sin():
    inv = 1.0 / (THETA ** (np.arange(0, HD, 2) / HD))
    ang = np.outer(np.arange(N), inv)
    return np.cos(ang), np.sin(ang)


def apply_rope(u, cos, sin):
    ur = u.reshape(B, N, H, HD // 2, 2)
    u0, u1 = ur[..., 0], ur[..., 1]
    c = cos[None, :, None, :]
    s = sin[None, :, None, :]
    return np.stack([u0 * c - u1 * s, u0 * s + u1 * c], axis=-1).reshape(B, N, H, HD)


def setup_inputs():
    s = mx_kscale(C)
    col = np.concatenate([np.full(2 * C, 0.9), np.full(C, 4.0)]) / np.sqrt(C)
    return {"x": bf(np.random.standard_normal((B, T, C)) * s),
            "short_term_memory": bf(np.random.standard_normal((B, S, C)) * s),
            "w_attn": bf(np.random.standard_normal((C, 3 * C)) * col / s[:, None])}


def reference(x, short_term_memory, w_attn):
    xcat = np.concatenate([f64(short_term_memory), f64(x)], axis=1)
    qkv = mxq(xcat, 2, "e4m3") @ mxq(f64(w_attn), 0, "e4m3")
    q, k, v = np.split(qkv, 3, axis=-1)
    q = q.reshape(B, N, H, HD)
    k = k.reshape(B, N, H, HD)
    v = v.reshape(B, N, H, HD)
    cos, sin = rope_cos_sin()
    return apply_rope(q, cos, sin), apply_rope(k, cos, sin), v

@@ -1,0 +1,258 @@
+import math
+from contextlib import ExitStack
+
+import concourse.mybir as mybir
+from concourse.masks import make_identity
+
+F32 = mybir.dt.float32
+BF16 = mybir.dt.bfloat16
+I32 = mybir.dt.int32
+U32 = mybir.dt.uint32
+U8 = mybir.dt.uint8
+FP8X4 = mybir.dt.float8_e4m3fn_x4
+ALU = mybir.AluOpType
+ACT = mybir.ActivationFunctionType
+
+P = 128
+PACK = 4
+BATCH = 4
+MEMORY = 256
+SEQ = 1024
+K = 512
+WORDS = K // 2
+BLOCK = 512
+HALF = BLOCK // 2
+HEADS = 4
+PAIRS = 64
+DOUBLINGS = 6
+THETA = 10000.0
+ROWS = 2
+CHUNK = P * ROWS
+CHUNKS_PER_SEQ = SEQ // CHUNK
+CHUNKS = BATCH * CHUNKS_PER_SEQ
+SLOTS = CHUNKS_PER_SEQ * ROWS
+Q_BLOCK, K_BLOCK, V_BLOCK = 0, 1, 2
+ROUND = 12582912.0
+
+FLOPS = 2 * BATCH * SEQ * K * 3 * BLOCK
+
+
+def build_rotation_tables(nc, pool):
+    position = pool.tile([P, SLOTS], I32)
+    nc.gpsimd.iota(
+        position[:],
+        pattern=[[CHUNK, CHUNKS_PER_SEQ], [1, ROWS]],
+        base=0,
+        channel_multiplier=ROWS,
+    )
+    position_f32 = pool.tile([P, SLOTS], F32)
+    nc.vector.tensor_copy(out=position_f32[:], in_=position[:])
+
+    frequency = pool.tile([P, PAIRS], F32)
+    nc.vector.memset(frequency[:, 0:1], 1.0)
+    for doubling in range(DOUBLINGS):
+        width = 2**doubling
+        nc.vector.tensor_scalar_mul(
+            out=frequency[:, width : 2 * width],
+            in0=frequency[:, 0:width],
+            scalar1=THETA ** (-width / PAIRS),
+        )
+
+    turns = pool.tile([P, 2, SLOTS, PAIRS], F32)
+    nc.vector.scalar_tensor_tensor(
+        out=turns[:, 0],
+        in0=position_f32[:].unsqueeze(2).to_broadcast([P, SLOTS, PAIRS]),
+        scalar=1.0 / (2.0 * math.pi),
+        in1=frequency[:].unsqueeze(1).to_broadcast([P, SLOTS, PAIRS]),
+        op0=ALU.mult,
+        op1=ALU.mult,
+    )
+    nc.vector.tensor_scalar_add(out=turns[:, 1], in0=turns[:, 0], scalar1=0.25)
+    whole = pool.tile([P, 2, SLOTS, PAIRS], F32)
+    nc.vector.tensor_scalar(
+        out=whole[:], in0=turns[:], scalar1=ROUND, scalar2=ROUND, op0=ALU.add, op1=ALU.subtract
+    )
+    fraction = pool.tile([P, 2, SLOTS, PAIRS], F32)
+    nc.vector.tensor_tensor(out=fraction[:], in0=turns[:], in1=whole[:], op=ALU.subtract)
+    sin_cos = pool.tile([P, 2, SLOTS, PAIRS], F32)
+    nc.scalar.activation(out=sin_cos[:], in_=fraction[:], func=ACT.Sin, scale=2.0 * math.pi)
+    sin = sin_cos[:, 0]
+    cos = sin_cos[:, 1]
+
+    partner = pool.tile([P, 2, SLOTS, PAIRS], F32)
+    nc.vector.scalar_tensor_tensor(
+        out=partner[:, 0], in0=cos, scalar=-1.0, in1=sin, op0=ALU.mult, op1=ALU.subtract
+    )
+    nc.vector.tensor_tensor(out=partner[:, 1], in0=sin, in1=cos, op=ALU.subtract)
+    return cos, partner
+
+
+def tile_memoryselfattention_pa_t_kernel(
+    tc, x, short_term_memory, w_attn, out_0, out_1, out_2
+):
+    nc = tc.nc
+    with ExitStack() as ctx:
+        keep = ctx.enter_context(tc.tile_pool(name="keep", bufs=1))
+        stage = ctx.enter_context(tc.tile_pool(name="stage", bufs=3))
+        results = ctx.enter_context(tc.tile_pool(name="results", bufs=6))
+        flipped_banks = ctx.enter_context(tc.psum_pool(name="flipped_banks", bufs=2))
+        product_banks = ctx.enter_context(tc.psum_pool(name="product_banks", bufs=6))
+
+        def chunk_rows(tensor_of_memory, tensor_of_x, chunk):
+            batch, part = divmod(chunk, CHUNKS_PER_SEQ)
+            if part == 0:
+                return tensor_of_memory[batch]
+            return tensor_of_x[batch, (part - 1) * CHUNK : part * CHUNK]
+
+        x_rows = [
+            keep.tile([P, ROWS, K], BF16, name="x_rows%d" % chunk) for chunk in range(CHUNKS)
+        ]
+        w_rows = keep.tile([P, 3, PACK, BLOCK], BF16)
+
+        def load_chunk(chunk):
+            nc.sync.dma_start(
+                out=x_rows[chunk][:],
+                in_=chunk_rows(short_term_memory, x, chunk).rearrange(
+                    "(p r) k -> p r k", r=ROWS
+                ),
+            )
+
+        def load_weight_block(block):
+            for u in range(2):
+                nc.sync.dma_start(
+                    out=w_rows[:, block, 2 * u : 2 * u + 2, :],
+                    in_=w_attn[
+                        WORDS * u : WORDS * (u + 1), BLOCK * block : BLOCK * (block + 1)
+                    ].rearrange("(p e) c -> p e c", e=2),
+                )
+
+        load_chunk(0)
+        load_weight_block(Q_BLOCK)
+        load_weight_block(K_BLOCK)
+        load_chunk(1)
+        load_weight_block(V_BLOCK)
+        for chunk in range(2, CHUNKS):
+            load_chunk(chunk)
+
+        cos, partner = build_rotation_tables(nc, keep)
+        identity = keep.tile([P, P], F32)
+        make_identity(nc, identity[:])
+
+        w_grouped = keep.tile([P, 3, 2, HALF, PACK], BF16, align_bytes=64)
+        w_codes = keep.tile([P, 3, BLOCK], U32, align_bytes=64)
+        w_scales = keep.tile([P, 3, BLOCK], U8, align_bytes=64)
+
+        def quantise_weight_block(block):
+            if block == V_BLOCK:
+                halves = w_rows[:, block].rearrange("p t (g n) -> p g n t", g=2)
+                first, second = halves[:, 0], halves[:, 1]
+            else:
+                parities = w_rows[:, block].rearrange("p t (n e) -> p e n t", e=2)
+                first, second = parities[:, 1], parities[:, 0]
+            nc.vector.tensor_copy(out=w_grouped[:, block, 0], in_=first)
+            nc.scalar.copy(out=w_grouped[:, block, 1], in_=second)
+            nc.vector.quantize_mx(
+                out=w_codes[:, block, :].bitcast(FP8X4),
+                scales=w_scales[:, block, :],
+                in_=w_grouped[:, block].rearrange("p g n t -> p (g n t)"),
+            )
+
+        def quantise_chunk(chunk):
+            words = x_rows[chunk][:].bitcast(F32)
+            flipped = flipped_banks.tile([P, ROWS, 2, P], F32)
+            for row in range(ROWS):
+                for u in range(2):
+                    nc.tensor.transpose(
+                        flipped[:, row, u, :], words[:, row, P * u : P * (u + 1)], identity[:]
+                    )
+            x_grouped = stage.tile([P, ROWS * P * PACK], BF16, align_bytes=64)
+            nc.scalar.copy(
+                out=x_grouped[:].bitcast(F32).rearrange("p (r m u) -> p r m u", r=ROWS, u=2),
+                in_=flipped[:].rearrange("p r u m -> p r m u"),
+            )
+            x_codes = stage.tile([P, ROWS * P], U32, align_bytes=64)
+            x_scales = stage.tile([P, ROWS * P], U8, align_bytes=64)
+            nc.vector.quantize_mx(
+                out=x_codes[:].bitcast(FP8X4), scales=x_scales[:], in_=x_grouped[:]
+            )
+            return x_codes, x_scales
+
+        def multiply(out, operand, row, block, first, last, start, stop):
+            x_codes, x_scales = operand
+            tokens = slice(P * row, P * (row + 1))
+            nc.tensor.matmul_mx(
+                out=out,
+                lhsT=x_codes[:, tokens].bitcast(FP8X4),
+                lhsT_scale=x_scales[:, tokens],
+                rhs=w_codes[:, block, first:last].bitcast(FP8X4),
+                rhs_scale=w_scales[:, block, first:last],
+                start=start,
+                stop=stop,
+            )
+
+        def project_and_rotate(chunk, operand, block, out):
+            part = chunk % CHUNKS_PER_SEQ
+            rotated = results.tile([P, ROWS, BLOCK], F32)
+            pair_sums = product_banks.tile([P, ROWS, HALF], F32, tag="bank")
+            for row in range(ROWS):
+                slot = part * ROWS + row
+                products = product_banks.tile([P, BLOCK], F32, tag="bank")
+                multiply(products[:], operand, row, block, 0, BLOCK, True, True)
+                multiply(pair_sums[:, row], operand, row, block, 0, HALF, True, False)
+                multiply(pair_sums[:, row], operand, row, block, HALF, BLOCK, False, True)
+                nc.vector.tensor_tensor(
+                    out=rotated[:, row].rearrange("p (h i e) -> p h i e", h=HEADS, e=2),
+                    in0=products[:].rearrange("p (e h i) -> p h i e", e=2, h=HEADS),
+                    in1=partner[:, :, slot, :]
+                    .rearrange("p e i -> p i e")
+                    .unsqueeze(1)
+                    .to_broadcast([P, HEADS, PAIRS, 2]),
+                    op=ALU.mult,
+                )
+            shared = results.tile([P, ROWS, HALF], F32)
+            nc.vector.tensor_tensor(
+                out=shared[:].rearrange("p r (h i) -> p r h i", h=HEADS),
+                in0=pair_sums[:].rearrange("p r (h i) -> p r h i", h=HEADS),
+                in1=cos[:, part * ROWS : (part + 1) * ROWS, :]
+                .unsqueeze(2)
+                .to_broadcast([P, ROWS, HEADS, PAIRS]),
+                op=ALU.mult,
+            )
+            pairs = rotated[:].rearrange("p r (n e) -> p (r n) e", e=2)
+            nc.gpsimd.tensor_tensor(
+                out=pairs,
+                in0=pairs,
+                in1=shared[:]
+                .rearrange("p r n -> p (r n)")
+                .unsqueeze(2)
+                .to_broadcast([P, ROWS * HALF, 2]),
+                op=ALU.add,
+            )
+            store(out, chunk, rotated)
+
+        def project(chunk, operand, out):
+            values = results.tile([P, ROWS, BLOCK], F32)
+            for row in range(ROWS):
+                products = product_banks.tile([P, BLOCK], F32, tag="bank")
+                multiply(products[:], operand, row, V_BLOCK, 0, BLOCK, True, True)
+                nc.scalar.copy(out=values[:, row], in_=products[:])
+            store(out, chunk, values)
+
+        def store(out, chunk, rows):
+            batch, part = divmod(chunk, CHUNKS_PER_SEQ)
+            nc.sync.dma_start(
+                out=out[batch, part * CHUNK : (part + 1) * CHUNK].rearrange(
+                    "(p r) h d -> p r (h d)", r=ROWS
+                ),
+                in_=rows[:],
+            )
+
+        operand = quantise_chunk(0)
+        for block in (Q_BLOCK, K_BLOCK, V_BLOCK):
+            quantise_weight_block(block)
+        for chunk in range(CHUNKS):
+            following = quantise_chunk(chunk + 1) if chunk + 1 < CHUNKS else None
+            project_and_rotate(chunk, operand, Q_BLOCK, out_0)
+            project_and_rotate(chunk, operand, K_BLOCK, out_1)
+            project(chunk, operand, out_2)
+            operand = following

@@ -32,6 +32,7 @@ CHUNKS_PER_SEQ = SEQ // CHUNK
 CHUNKS = BATCH * CHUNKS_PER_SEQ
 SLOTS = CHUNKS_PER_SEQ * ROWS
 Q_BLOCK, K_BLOCK, V_BLOCK = 0, 1, 2
+VECTOR_PAIRS = 160
 ROUND = 12582912.0
 
 FLOPS = 2 * BATCH * SEQ * K * 3 * BLOCK
@@ -150,7 +151,10 @@ def tile_memoryselfattention_pa_t_kernel(
                 parities = w_rows[:, block].rearrange("p t (n e) -> p e n t", e=2)
                 first, second = parities[:, 1], parities[:, 0]
             nc.vector.tensor_copy(out=w_grouped[:, block, 0], in_=first)
-            nc.scalar.copy(out=w_grouped[:, block, 1], in_=second)
+            if block == Q_BLOCK:
+                nc.vector.tensor_copy(out=w_grouped[:, block, 1], in_=second)
+            else:
+                nc.scalar.copy(out=w_grouped[:, block, 1], in_=second)
             nc.vector.quantize_mx(
                 out=w_codes[:, block, :].bitcast(FP8X4),
                 scales=w_scales[:, block, :],
@@ -219,13 +223,18 @@ def tile_memoryselfattention_pa_t_kernel(
                 op=ALU.mult,
             )
             pairs = rotated[:].rearrange("p r (n e) -> p (r n) e", e=2)
+            sums = shared[:].rearrange("p r n -> p (r n)").unsqueeze(2)
+            split = ROWS * HALF - VECTOR_PAIRS
             nc.gpsimd.tensor_tensor(
-                out=pairs,
-                in0=pairs,
-                in1=shared[:]
-                .rearrange("p r n -> p (r n)")
-                .unsqueeze(2)
-                .to_broadcast([P, ROWS * HALF, 2]),
+                out=pairs[:, 0:split],
+                in0=pairs[:, 0:split],
+                in1=sums[:, 0:split].to_broadcast([P, split, 2]),
+                op=ALU.add,
+            )
+            nc.vector.tensor_tensor(
+                out=pairs[:, split:],
+                in0=pairs[:, split:],
+                in1=sums[:, split:].to_broadcast([P, VECTOR_PAIRS, 2]),
                 op=ALU.add,
             )
             store(out, chunk, rotated)
@@ -248,11 +257,14 @@ def tile_memoryselfattention_pa_t_kernel(
             )
 
         operand = quantise_chunk(0)
-        for block in (Q_BLOCK, K_BLOCK, V_BLOCK):
-            quantise_weight_block(block)
+        quantise_weight_block(Q_BLOCK)
         for chunk in range(CHUNKS):
-            following = quantise_chunk(chunk + 1) if chunk + 1 < CHUNKS else None
             project_and_rotate(chunk, operand, Q_BLOCK, out_0)
+            if chunk == 0:
+                quantise_weight_block(K_BLOCK)
+            following = quantise_chunk(chunk + 1) if chunk + 1 < CHUNKS else None
             project_and_rotate(chunk, operand, K_BLOCK, out_1)
+            if chunk == 0:
+                quantise_weight_block(V_BLOCK)
             project(chunk, operand, out_2)
             operand = following

@@ -16,7 +16,6 @@ ACT = mybir.ActivationFunctionType
 P = 128
 PACK = 4
 BATCH = 4
-MEMORY = 256
 SEQ = 1024
 K = 512
 WORDS = K // 2
@@ -32,13 +31,12 @@ CHUNKS_PER_SEQ = SEQ // CHUNK
 CHUNKS = BATCH * CHUNKS_PER_SEQ
 SLOTS = CHUNKS_PER_SEQ * ROWS
 Q_BLOCK, K_BLOCK, V_BLOCK = 0, 1, 2
-VECTOR_PAIRS = 160
 ROUND = 12582912.0
 
 FLOPS = 2 * BATCH * SEQ * K * 3 * BLOCK
 
 
-def build_rotation_tables(nc, pool):
+def build_sin_cos(nc, pool):
     position = pool.tile([P, SLOTS], I32)
     nc.gpsimd.iota(
         position[:],
@@ -77,15 +75,16 @@ def build_rotation_tables(nc, pool):
     nc.vector.tensor_tensor(out=fraction[:], in0=turns[:], in1=whole[:], op=ALU.subtract)
     sin_cos = pool.tile([P, 2, SLOTS, PAIRS], F32)
     nc.scalar.activation(out=sin_cos[:], in_=fraction[:], func=ACT.Sin, scale=2.0 * math.pi)
-    sin = sin_cos[:, 0]
-    cos = sin_cos[:, 1]
+    return sin_cos
 
-    partner = pool.tile([P, 2, SLOTS, PAIRS], F32)
+
+def build_partner_factors(nc, pool, sin, cos):
+    factors = pool.tile([P, 2, SLOTS, PAIRS], F32)
     nc.vector.scalar_tensor_tensor(
-        out=partner[:, 0], in0=cos, scalar=-1.0, in1=sin, op0=ALU.mult, op1=ALU.subtract
+        out=factors[:, 0], in0=cos, scalar=-1.0, in1=sin, op0=ALU.mult, op1=ALU.subtract
     )
-    nc.vector.tensor_tensor(out=partner[:, 1], in0=sin, in1=cos, op=ALU.subtract)
-    return cos, partner
+    nc.vector.tensor_tensor(out=factors[:, 1], in0=sin, in1=cos, op=ALU.subtract)
+    return factors
 
 
 def tile_memoryselfattention_pa_t_kernel(
@@ -97,13 +96,9 @@ def tile_memoryselfattention_pa_t_kernel(
         stage = ctx.enter_context(tc.tile_pool(name="stage", bufs=3))
         results = ctx.enter_context(tc.tile_pool(name="results", bufs=6))
         flipped_banks = ctx.enter_context(tc.psum_pool(name="flipped_banks", bufs=2))
-        product_banks = ctx.enter_context(tc.psum_pool(name="product_banks", bufs=6))
-
-        def chunk_rows(tensor_of_memory, tensor_of_x, chunk):
-            batch, part = divmod(chunk, CHUNKS_PER_SEQ)
-            if part == 0:
-                return tensor_of_memory[batch]
-            return tensor_of_x[batch, (part - 1) * CHUNK : part * CHUNK]
+        sum_banks = ctx.enter_context(tc.psum_pool(name="sum_banks", bufs=2))
+        product_banks = ctx.enter_context(tc.psum_pool(name="product_banks", bufs=4))
+        ctx.enter_context(tc.manual_schedule())
 
         x_rows = [
             keep.tile([P, ROWS, K], BF16, name="x_rows%d" % chunk) for chunk in range(CHUNKS)
@@ -111,11 +106,13 @@ def tile_memoryselfattention_pa_t_kernel(
         w_rows = keep.tile([P, 3, PACK, BLOCK], BF16)
 
         def load_chunk(chunk):
+            batch, part = divmod(chunk, CHUNKS_PER_SEQ)
+            if part == 0:
+                rows = short_term_memory[batch]
+            else:
+                rows = x[batch, (part - 1) * CHUNK : part * CHUNK]
             nc.sync.dma_start(
-                out=x_rows[chunk][:],
-                in_=chunk_rows(short_term_memory, x, chunk).rearrange(
-                    "(p r) k -> p r k", r=ROWS
-                ),
+                out=x_rows[chunk][:], in_=rows.rearrange("(p r) k -> p r k", r=ROWS)
             )
 
         def load_weight_block(block):
@@ -135,15 +132,11 @@ def tile_memoryselfattention_pa_t_kernel(
         for chunk in range(2, CHUNKS):
             load_chunk(chunk)
 
-        cos, partner = build_rotation_tables(nc, keep)
-        identity = keep.tile([P, P], F32)
-        make_identity(nc, identity[:])
-
         w_grouped = keep.tile([P, 3, 2, HALF, PACK], BF16, align_bytes=64)
         w_codes = keep.tile([P, 3, BLOCK], U32, align_bytes=64)
         w_scales = keep.tile([P, 3, BLOCK], U8, align_bytes=64)
 
-        def quantise_weight_block(block):
+        def regroup_weight_block(block, copy_second_half):
             if block == V_BLOCK:
                 halves = w_rows[:, block].rearrange("p t (g n) -> p g n t", g=2)
                 first, second = halves[:, 0], halves[:, 1]
@@ -151,17 +144,19 @@ def tile_memoryselfattention_pa_t_kernel(
                 parities = w_rows[:, block].rearrange("p t (n e) -> p e n t", e=2)
                 first, second = parities[:, 1], parities[:, 0]
             nc.vector.tensor_copy(out=w_grouped[:, block, 0], in_=first)
-            if block == Q_BLOCK:
-                nc.vector.tensor_copy(out=w_grouped[:, block, 1], in_=second)
-            else:
-                nc.scalar.copy(out=w_grouped[:, block, 1], in_=second)
+            copy_second_half(out=w_grouped[:, block, 1], in_=second)
+
+        def quantise_weight_block(block):
             nc.vector.quantize_mx(
                 out=w_codes[:, block, :].bitcast(FP8X4),
                 scales=w_scales[:, block, :],
                 in_=w_grouped[:, block].rearrange("p g n t -> p (g n t)"),
             )
 
-        def quantise_chunk(chunk):
+        x_grouped = {}
+        x_operands = {}
+
+        def flip_chunk(chunk):
             words = x_rows[chunk][:].bitcast(F32)
             flipped = flipped_banks.tile([P, ROWS, 2, P], F32)
             for row in range(ROWS):
@@ -169,83 +164,33 @@ def tile_memoryselfattention_pa_t_kernel(
                     nc.tensor.transpose(
                         flipped[:, row, u, :], words[:, row, P * u : P * (u + 1)], identity[:]
                     )
-            x_grouped = stage.tile([P, ROWS * P * PACK], BF16, align_bytes=64)
+            grouped = stage.tile([P, ROWS * P * PACK], BF16, align_bytes=64)
             nc.scalar.copy(
-                out=x_grouped[:].bitcast(F32).rearrange("p (r m u) -> p r m u", r=ROWS, u=2),
+                out=grouped[:].bitcast(F32).rearrange("p (r m u) -> p r m u", r=ROWS, u=2),
                 in_=flipped[:].rearrange("p r u m -> p r m u"),
             )
-            x_codes = stage.tile([P, ROWS * P], U32, align_bytes=64)
-            x_scales = stage.tile([P, ROWS * P], U8, align_bytes=64)
-            nc.vector.quantize_mx(
-                out=x_codes[:].bitcast(FP8X4), scales=x_scales[:], in_=x_grouped[:]
-            )
-            return x_codes, x_scales
+            x_grouped[chunk] = grouped
 
-        def multiply(out, operand, row, block, first, last, start, stop):
-            x_codes, x_scales = operand
+        def quantise_chunk(chunk):
+            codes = stage.tile([P, ROWS * P], U32, align_bytes=64)
+            scales = stage.tile([P, ROWS * P], U8, align_bytes=64)
+            nc.vector.quantize_mx(
+                out=codes[:].bitcast(FP8X4), scales=scales[:], in_=x_grouped[chunk][:]
+            )
+            x_operands[chunk] = (codes, scales)
+
+        def multiply(out, chunk, row, block, first, last, start, stop):
+            codes, scales = x_operands[chunk]
             tokens = slice(P * row, P * (row + 1))
             nc.tensor.matmul_mx(
                 out=out,
-                lhsT=x_codes[:, tokens].bitcast(FP8X4),
-                lhsT_scale=x_scales[:, tokens],
+                lhsT=codes[:, tokens].bitcast(FP8X4),
+                lhsT_scale=scales[:, tokens],
                 rhs=w_codes[:, block, first:last].bitcast(FP8X4),
                 rhs_scale=w_scales[:, block, first:last],
                 start=start,
                 stop=stop,
             )
-
-        def project_and_rotate(chunk, operand, block, out):
-            part = chunk % CHUNKS_PER_SEQ
-            rotated = results.tile([P, ROWS, BLOCK], F32)
-            pair_sums = product_banks.tile([P, ROWS, HALF], F32, tag="bank")
-            for row in range(ROWS):
-                slot = part * ROWS + row
-                products = product_banks.tile([P, BLOCK], F32, tag="bank")
-                multiply(products[:], operand, row, block, 0, BLOCK, True, True)
-                multiply(pair_sums[:, row], operand, row, block, 0, HALF, True, False)
-                multiply(pair_sums[:, row], operand, row, block, HALF, BLOCK, False, True)
-                nc.vector.tensor_tensor(
-                    out=rotated[:, row].rearrange("p (h i e) -> p h i e", h=HEADS, e=2),
-                    in0=products[:].rearrange("p (e h i) -> p h i e", e=2, h=HEADS),
-                    in1=partner[:, :, slot, :]
-                    .rearrange("p e i -> p i e")
-                    .unsqueeze(1)
-                    .to_broadcast([P, HEADS, PAIRS, 2]),
-                    op=ALU.mult,
-                )
-            shared = results.tile([P, ROWS, HALF], F32)
-            nc.vector.tensor_tensor(
-                out=shared[:].rearrange("p r (h i) -> p r h i", h=HEADS),
-                in0=pair_sums[:].rearrange("p r (h i) -> p r h i", h=HEADS),
-                in1=cos[:, part * ROWS : (part + 1) * ROWS, :]
-                .unsqueeze(2)
-                .to_broadcast([P, ROWS, HEADS, PAIRS]),
-                op=ALU.mult,
-            )
-            pairs = rotated[:].rearrange("p r (n e) -> p (r n) e", e=2)
-            sums = shared[:].rearrange("p r n -> p (r n)").unsqueeze(2)
-            split = ROWS * HALF - VECTOR_PAIRS
-            nc.gpsimd.tensor_tensor(
-                out=pairs[:, 0:split],
-                in0=pairs[:, 0:split],
-                in1=sums[:, 0:split].to_broadcast([P, split, 2]),
-                op=ALU.add,
-            )
-            nc.vector.tensor_tensor(
-                out=pairs[:, split:],
-                in0=pairs[:, split:],
-                in1=sums[:, split:].to_broadcast([P, VECTOR_PAIRS, 2]),
-                op=ALU.add,
-            )
-            store(out, chunk, rotated)
-
-        def project(chunk, operand, out):
-            values = results.tile([P, ROWS, BLOCK], F32)
-            for row in range(ROWS):
-                products = product_banks.tile([P, BLOCK], F32, tag="bank")
-                multiply(products[:], operand, row, V_BLOCK, 0, BLOCK, True, True)
-                nc.scalar.copy(out=values[:, row], in_=products[:])
-            store(out, chunk, values)
 
         def store(out, chunk, rows):
             batch, part = divmod(chunk, CHUNKS_PER_SEQ)
@@ -256,15 +201,91 @@ def tile_memoryselfattention_pa_t_kernel(
                 in_=rows[:],
             )
 
-        operand = quantise_chunk(0)
+        def partner_products(chunk, block):
+            part = chunk % CHUNKS_PER_SEQ
+            rotated = results.tile([P, ROWS, BLOCK], F32)
+            pair_sums = sum_banks.tile([P, ROWS, HALF], F32)
+            for row in range(ROWS):
+                products = product_banks.tile([P, BLOCK], F32)
+                multiply(products[:], chunk, row, block, 0, BLOCK, True, True)
+                multiply(pair_sums[:, row], chunk, row, block, 0, HALF, True, False)
+                multiply(pair_sums[:, row], chunk, row, block, HALF, BLOCK, False, True)
+                nc.vector.tensor_tensor(
+                    out=rotated[:, row].rearrange("p (h i e) -> p h i e", h=HEADS, e=2),
+                    in0=products[:].rearrange("p (e h i) -> p h i e", e=2, h=HEADS),
+                    in1=partner_factors[:, :, part * ROWS + row, :]
+                    .rearrange("p e i -> p i e")
+                    .unsqueeze(1)
+                    .to_broadcast([P, HEADS, PAIRS, 2]),
+                    op=ALU.mult,
+                )
+            return rotated, pair_sums
+
+        def shared_products(chunk, pair_sums):
+            part = chunk % CHUNKS_PER_SEQ
+            shared = results.tile([P, ROWS, HALF], F32)
+            nc.vector.tensor_tensor(
+                out=shared[:].rearrange("p r (h i) -> p r h i", h=HEADS),
+                in0=pair_sums[:].rearrange("p r (h i) -> p r h i", h=HEADS),
+                in1=cos[:, part * ROWS : (part + 1) * ROWS, :]
+                .unsqueeze(2)
+                .to_broadcast([P, ROWS, HEADS, PAIRS]),
+                op=ALU.mult,
+            )
+            return shared
+
+        def add_shared(engine, rotated, shared):
+            pairs = rotated[:].rearrange("p r (n e) -> p (r n) e", e=2)
+            engine.tensor_tensor(
+                out=pairs,
+                in0=pairs,
+                in1=shared[:]
+                .rearrange("p r n -> p (r n)")
+                .unsqueeze(2)
+                .to_broadcast([P, ROWS * HALF, 2]),
+                op=ALU.add,
+            )
+
+        def project_values(chunk):
+            values = results.tile([P, ROWS, BLOCK], F32)
+            for row in range(ROWS):
+                products = product_banks.tile([P, BLOCK], F32)
+                multiply(products[:], chunk, row, V_BLOCK, 0, BLOCK, True, True)
+                nc.scalar.copy(out=values[:, row], in_=products[:])
+            store(out_2, chunk, values)
+
+        sin_cos = build_sin_cos(nc, keep)
+        sin = sin_cos[:, 0]
+        cos = sin_cos[:, 1]
+        identity = keep.tile([P, P], F32)
+        make_identity(nc, identity[:])
+        flip_chunk(0)
+        regroup_weight_block(Q_BLOCK, nc.vector.tensor_copy)
+        partner_factors = build_partner_factors(nc, keep, sin, cos)
         quantise_weight_block(Q_BLOCK)
+        quantise_chunk(0)
+        regroup_weight_block(K_BLOCK, nc.scalar.copy)
+        regroup_weight_block(V_BLOCK, nc.scalar.copy)
+        flip_chunk(1)
+        quantise_weight_block(K_BLOCK)
+        quantise_weight_block(V_BLOCK)
+        quantise_chunk(1)
+
+        q_rotated, q_sums = partner_products(0, Q_BLOCK)
+        q_shared = shared_products(0, q_sums)
         for chunk in range(CHUNKS):
-            project_and_rotate(chunk, operand, Q_BLOCK, out_0)
-            if chunk == 0:
-                quantise_weight_block(K_BLOCK)
-            following = quantise_chunk(chunk + 1) if chunk + 1 < CHUNKS else None
-            project_and_rotate(chunk, operand, K_BLOCK, out_1)
-            if chunk == 0:
-                quantise_weight_block(V_BLOCK)
-            project(chunk, operand, out_2)
-            operand = following
+            add_shared(nc.gpsimd, q_rotated, q_shared)
+            store(out_0, chunk, q_rotated)
+            k_rotated, k_sums = partner_products(chunk, K_BLOCK)
+            k_shared = shared_products(chunk, k_sums)
+            project_values(chunk)
+            if chunk + 2 < CHUNKS:
+                flip_chunk(chunk + 2)
+            if chunk + 1 < CHUNKS:
+                q_rotated, q_sums = partner_products(chunk + 1, Q_BLOCK)
+            add_shared(nc.vector, k_rotated, k_shared)
+            store(out_1, chunk, k_rotated)
+            if chunk + 2 < CHUNKS:
+                quantise_chunk(chunk + 2)
+            if chunk + 1 < CHUNKS:
+                q_shared = shared_products(chunk + 1, q_sums)

@@ -201,9 +201,8 @@ def tile_memoryselfattention_pa_t_kernel(
                 in_=rows[:],
             )
 
-        def partner_products(chunk, block):
+        def partner_products(chunk, block, outs):
             part = chunk % CHUNKS_PER_SEQ
-            rotated = results.tile([P, ROWS, BLOCK], F32)
             pair_sums = sum_banks.tile([P, ROWS, HALF], F32)
             for row in range(ROWS):
                 products = product_banks.tile([P, BLOCK], F32)
@@ -211,7 +210,7 @@ def tile_memoryselfattention_pa_t_kernel(
                 multiply(pair_sums[:, row], chunk, row, block, 0, HALF, True, False)
                 multiply(pair_sums[:, row], chunk, row, block, HALF, BLOCK, False, True)
                 nc.vector.tensor_tensor(
-                    out=rotated[:, row].rearrange("p (h i e) -> p h i e", h=HEADS, e=2),
+                    out=outs[row].rearrange("p (h i e) -> p h i e", h=HEADS, e=2),
                     in0=products[:].rearrange("p (e h i) -> p h i e", e=2, h=HEADS),
                     in1=partner_factors[:, :, part * ROWS + row, :]
                     .rearrange("p e i -> p i e")
@@ -219,7 +218,7 @@ def tile_memoryselfattention_pa_t_kernel(
                     .to_broadcast([P, HEADS, PAIRS, 2]),
                     op=ALU.mult,
                 )
-            return rotated, pair_sums
+            return pair_sums
 
         def shared_products(chunk, pair_sums):
             part = chunk % CHUNKS_PER_SEQ
@@ -234,15 +233,12 @@ def tile_memoryselfattention_pa_t_kernel(
             )
             return shared
 
-        def add_shared(engine, rotated, shared):
-            pairs = rotated[:].rearrange("p r (n e) -> p (r n) e", e=2)
+        def add_shared(engine, out, products, shared):
+            pairs = shared.shape[1]
             engine.tensor_tensor(
-                out=pairs,
-                in0=pairs,
-                in1=shared[:]
-                .rearrange("p r n -> p (r n)")
-                .unsqueeze(2)
-                .to_broadcast([P, ROWS * HALF, 2]),
+                out=out.rearrange("p (n e) -> p n e", e=2),
+                in0=products.rearrange("p (n e) -> p n e", e=2),
+                in1=shared.unsqueeze(2).to_broadcast([P, pairs, 2]),
                 op=ALU.add,
             )
 
@@ -271,21 +267,30 @@ def tile_memoryselfattention_pa_t_kernel(
         quantise_weight_block(V_BLOCK)
         quantise_chunk(1)
 
-        q_rotated, q_sums = partner_products(0, Q_BLOCK)
+        def start_q(chunk):
+            q_rotated = results.tile([P, ROWS, BLOCK], F32)
+            q_sums = partner_products(chunk, Q_BLOCK, [q_rotated[:, row] for row in range(ROWS)])
+            return q_rotated, q_sums
+
+        q_rotated, q_sums = start_q(0)
         q_shared = shared_products(0, q_sums)
         for chunk in range(CHUNKS):
-            add_shared(nc.gpsimd, q_rotated, q_shared)
+            q_flat = q_rotated[:].rearrange("p r n -> p (r n)")
+            add_shared(nc.gpsimd, q_flat, q_flat, q_shared[:].rearrange("p r n -> p (r n)"))
             store(out_0, chunk, q_rotated)
-            k_rotated, k_sums = partner_products(chunk, K_BLOCK)
+            k_rotated = results.tile([P, ROWS, BLOCK], F32)
+            k_first = results.tile([P, BLOCK], F32)
+            k_sums = partner_products(chunk, K_BLOCK, [k_first[:], k_rotated[:, 0]])
             k_shared = shared_products(chunk, k_sums)
             project_values(chunk)
             if chunk + 2 < CHUNKS:
                 flip_chunk(chunk + 2)
             if chunk + 1 < CHUNKS:
-                q_rotated, q_sums = partner_products(chunk + 1, Q_BLOCK)
-            add_shared(nc.vector, k_rotated, k_shared)
-            store(out_1, chunk, k_rotated)
+                q_rotated, q_sums = start_q(chunk + 1)
             if chunk + 2 < CHUNKS:
                 quantise_chunk(chunk + 2)
+            add_shared(nc.vector, k_rotated[:, 1], k_rotated[:, 0], k_shared[:, 1])
+            add_shared(nc.gpsimd, k_rotated[:, 0], k_first[:], k_shared[:, 0])
+            store(out_1, chunk, k_rotated)
             if chunk + 1 < CHUNKS:
                 q_shared = shared_products(chunk + 1, q_sums)

@@ -31,12 +31,13 @@ CHUNKS_PER_SEQ = SEQ // CHUNK
 CHUNKS = BATCH * CHUNKS_PER_SEQ
 SLOTS = CHUNKS_PER_SEQ * ROWS
 Q_BLOCK, K_BLOCK, V_BLOCK = 0, 1, 2
+K_BY_GPSIMD = 256
 ROUND = 12582912.0
 
 FLOPS = 2 * BATCH * SEQ * K * 3 * BLOCK
 
 
-def build_sin_cos(nc, pool):
+def build_positions(nc, pool):
     position = pool.tile([P, SLOTS], I32)
     nc.gpsimd.iota(
         position[:],
@@ -46,7 +47,10 @@ def build_sin_cos(nc, pool):
     )
     position_f32 = pool.tile([P, SLOTS], F32)
     nc.vector.tensor_copy(out=position_f32[:], in_=position[:])
+    return position_f32
 
+
+def build_frequencies(nc, pool):
     frequency = pool.tile([P, PAIRS], F32)
     nc.vector.memset(frequency[:, 0:1], 1.0)
     for doubling in range(DOUBLINGS):
@@ -56,35 +60,55 @@ def build_sin_cos(nc, pool):
             in0=frequency[:, 0:width],
             scalar1=THETA ** (-width / PAIRS),
         )
-
-    turns = pool.tile([P, 2, SLOTS, PAIRS], F32)
-    nc.vector.scalar_tensor_tensor(
-        out=turns[:, 0],
-        in0=position_f32[:].unsqueeze(2).to_broadcast([P, SLOTS, PAIRS]),
-        scalar=1.0 / (2.0 * math.pi),
-        in1=frequency[:].unsqueeze(1).to_broadcast([P, SLOTS, PAIRS]),
-        op0=ALU.mult,
-        op1=ALU.mult,
-    )
-    nc.vector.tensor_scalar_add(out=turns[:, 1], in0=turns[:, 0], scalar1=0.25)
-    whole = pool.tile([P, 2, SLOTS, PAIRS], F32)
-    nc.vector.tensor_scalar(
-        out=whole[:], in0=turns[:], scalar1=ROUND, scalar2=ROUND, op0=ALU.add, op1=ALU.subtract
-    )
-    fraction = pool.tile([P, 2, SLOTS, PAIRS], F32)
-    nc.vector.tensor_tensor(out=fraction[:], in0=turns[:], in1=whole[:], op=ALU.subtract)
-    sin_cos = pool.tile([P, 2, SLOTS, PAIRS], F32)
-    nc.scalar.activation(out=sin_cos[:], in_=fraction[:], func=ACT.Sin, scale=2.0 * math.pi)
-    return sin_cos
+    return frequency
 
 
-def build_partner_factors(nc, pool, sin, cos):
-    factors = pool.tile([P, 2, SLOTS, PAIRS], F32)
-    nc.vector.scalar_tensor_tensor(
-        out=factors[:, 0], in0=cos, scalar=-1.0, in1=sin, op0=ALU.mult, op1=ALU.subtract
-    )
-    nc.vector.tensor_tensor(out=factors[:, 1], in0=sin, in1=cos, op=ALU.subtract)
-    return factors
+def angle_steps(nc, pool, position, frequency):
+    slots = position.shape[1]
+    turns = pool.tile([P, slots, PAIRS], F32, name="turns%d" % slots)
+    whole = pool.tile([P, slots, PAIRS], F32, name="whole%d" % slots)
+    fraction = pool.tile([P, slots, PAIRS], F32, name="fraction%d" % slots)
+
+    def multiply_out():
+        nc.vector.scalar_tensor_tensor(
+            out=turns[:],
+            in0=position.unsqueeze(2).to_broadcast([P, slots, PAIRS]),
+            scalar=1.0 / (2.0 * math.pi),
+            in1=frequency[:].unsqueeze(1).to_broadcast([P, slots, PAIRS]),
+            op0=ALU.mult,
+            op1=ALU.mult,
+        )
+
+    def round_off():
+        nc.vector.tensor_scalar(
+            out=whole[:], in0=turns[:], scalar1=ROUND, scalar2=ROUND, op0=ALU.add, op1=ALU.subtract
+        )
+
+    def take_away():
+        nc.vector.tensor_tensor(out=fraction[:], in0=turns[:], in1=whole[:], op=ALU.subtract)
+
+    return (multiply_out, round_off, take_away), fraction
+
+
+def build_factors(nc, factors, half_sines, turns, first_slot):
+    slots = slice(first_slot, first_slot + ROWS)
+    for plane, shift in enumerate((-0.125, 0.125, 0.0)):
+        nc.scalar.activation(
+            out=half_sines[:, plane, slots],
+            in_=turns,
+            func=ACT.Sin,
+            scale=math.pi,
+            bias=shift * math.pi,
+        )
+    nc.scalar.square(half_sines[:, :, slots], half_sines[:, :, slots])
+    for first, last, size in ((0, 2, -math.sqrt(2.0)), (2, 3, 1.0)):
+        nc.scalar.activation(
+            out=factors[:, first:last, slots],
+            in_=half_sines[:, first:last, slots],
+            func=ACT.Copy,
+            scale=-2.0 * size,
+            bias=size,
+        )
 
 
 def tile_memoryselfattention_pa_t_kernel(
@@ -93,7 +117,7 @@ def tile_memoryselfattention_pa_t_kernel(
     nc = tc.nc
     with ExitStack() as ctx:
         keep = ctx.enter_context(tc.tile_pool(name="keep", bufs=1))
-        stage = ctx.enter_context(tc.tile_pool(name="stage", bufs=3))
+        stage = ctx.enter_context(tc.tile_pool(name="stage", bufs=4))
         results = ctx.enter_context(tc.tile_pool(name="results", bufs=6))
         flipped_banks = ctx.enter_context(tc.psum_pool(name="flipped_banks", bufs=2))
         sum_banks = ctx.enter_context(tc.psum_pool(name="sum_banks", bufs=2))
@@ -106,7 +130,7 @@ def tile_memoryselfattention_pa_t_kernel(
         w_rows = keep.tile([P, 3, PACK, BLOCK], BF16)
 
         def load_chunk(chunk):
-            batch, part = divmod(chunk, CHUNKS_PER_SEQ)
+            part, batch = divmod(chunk, BATCH)
             if part == 0:
                 rows = short_term_memory[batch]
             else:
@@ -124,10 +148,10 @@ def tile_memoryselfattention_pa_t_kernel(
                     ].rearrange("(p e) c -> p e c", e=2),
                 )
 
-        load_chunk(0)
         load_weight_block(Q_BLOCK)
-        load_weight_block(K_BLOCK)
+        load_chunk(0)
         load_chunk(1)
+        load_weight_block(K_BLOCK)
         load_weight_block(V_BLOCK)
         for chunk in range(2, CHUNKS):
             load_chunk(chunk)
@@ -136,14 +160,14 @@ def tile_memoryselfattention_pa_t_kernel(
         w_codes = keep.tile([P, 3, BLOCK], U32, align_bytes=64)
         w_scales = keep.tile([P, 3, BLOCK], U8, align_bytes=64)
 
-        def regroup_weight_block(block, copy_second_half):
+        def regroup_weight_block(block, copy_first_half, copy_second_half):
             if block == V_BLOCK:
                 halves = w_rows[:, block].rearrange("p t (g n) -> p g n t", g=2)
                 first, second = halves[:, 0], halves[:, 1]
             else:
                 parities = w_rows[:, block].rearrange("p t (n e) -> p e n t", e=2)
                 first, second = parities[:, 1], parities[:, 0]
-            nc.vector.tensor_copy(out=w_grouped[:, block, 0], in_=first)
+            copy_first_half(out=w_grouped[:, block, 0], in_=first)
             copy_second_half(out=w_grouped[:, block, 1], in_=second)
 
         def quantise_weight_block(block):
@@ -192,17 +216,18 @@ def tile_memoryselfattention_pa_t_kernel(
                 stop=stop,
             )
 
-        def store(out, chunk, rows):
-            batch, part = divmod(chunk, CHUNKS_PER_SEQ)
+        def store(out, chunk, tokens, first_row=0, last_row=ROWS):
+            part, batch = divmod(chunk, BATCH)
+            rows = slice(first_row, last_row)
             nc.sync.dma_start(
                 out=out[batch, part * CHUNK : (part + 1) * CHUNK].rearrange(
                     "(p r) h d -> p r (h d)", r=ROWS
-                ),
-                in_=rows[:],
+                )[:, rows],
+                in_=tokens.rearrange("p (r n) -> p r n", r=ROWS)[:, rows],
             )
 
-        def partner_products(chunk, block, outs):
-            part = chunk % CHUNKS_PER_SEQ
+        def partner_products(out, chunk, block):
+            part = chunk // BATCH
             pair_sums = sum_banks.tile([P, ROWS, HALF], F32)
             for row in range(ROWS):
                 products = product_banks.tile([P, BLOCK], F32)
@@ -210,9 +235,11 @@ def tile_memoryselfattention_pa_t_kernel(
                 multiply(pair_sums[:, row], chunk, row, block, 0, HALF, True, False)
                 multiply(pair_sums[:, row], chunk, row, block, HALF, BLOCK, False, True)
                 nc.vector.tensor_tensor(
-                    out=outs[row].rearrange("p (h i e) -> p h i e", h=HEADS, e=2),
+                    out=out[:, BLOCK * row : BLOCK * (row + 1)].rearrange(
+                        "p (h i e) -> p h i e", h=HEADS, e=2
+                    ),
                     in0=products[:].rearrange("p (e h i) -> p h i e", e=2, h=HEADS),
-                    in1=partner_factors[:, :, part * ROWS + row, :]
+                    in1=factors[:, 0:2, part * ROWS + row, :]
                     .rearrange("p e i -> p i e")
                     .unsqueeze(1)
                     .to_broadcast([P, HEADS, PAIRS, 2]),
@@ -220,77 +247,103 @@ def tile_memoryselfattention_pa_t_kernel(
                 )
             return pair_sums
 
-        def shared_products(chunk, pair_sums):
-            part = chunk % CHUNKS_PER_SEQ
-            shared = results.tile([P, ROWS, HALF], F32)
+        def shared_products(out, chunk, pair_sums):
+            part = chunk // BATCH
             nc.vector.tensor_tensor(
-                out=shared[:].rearrange("p r (h i) -> p r h i", h=HEADS),
+                out=out.rearrange("p (r h i) -> p r h i", r=ROWS, h=HEADS),
                 in0=pair_sums[:].rearrange("p r (h i) -> p r h i", h=HEADS),
-                in1=cos[:, part * ROWS : (part + 1) * ROWS, :]
+                in1=factors[:, 2, part * ROWS : (part + 1) * ROWS, :]
                 .unsqueeze(2)
                 .to_broadcast([P, ROWS, HEADS, PAIRS]),
                 op=ALU.mult,
             )
-            return shared
 
-        def add_shared(engine, out, products, shared):
-            pairs = shared.shape[1]
+        def add_shared(engine, out, products, shared, first, last):
             engine.tensor_tensor(
-                out=out.rearrange("p (n e) -> p n e", e=2),
-                in0=products.rearrange("p (n e) -> p n e", e=2),
-                in1=shared.unsqueeze(2).to_broadcast([P, pairs, 2]),
+                out=out[:, first:last].rearrange("p (n e) -> p n e", e=2),
+                in0=products[:, first:last].rearrange("p (n e) -> p n e", e=2),
+                in1=shared[:, first // 2 : last // 2]
+                .unsqueeze(2)
+                .to_broadcast([P, (last - first) // 2, 2]),
                 op=ALU.add,
             )
 
         def project_values(chunk):
-            values = results.tile([P, ROWS, BLOCK], F32)
+            values = results.tile([P, ROWS * BLOCK], F32)
             for row in range(ROWS):
                 products = product_banks.tile([P, BLOCK], F32)
                 multiply(products[:], chunk, row, V_BLOCK, 0, BLOCK, True, True)
-                nc.scalar.copy(out=values[:, row], in_=products[:])
-            store(out_2, chunk, values)
+                nc.scalar.copy(
+                    out=values[:, BLOCK * row : BLOCK * (row + 1)], in_=products[:]
+                )
+            store(out_2, chunk, values[:])
 
-        sin_cos = build_sin_cos(nc, keep)
-        sin = sin_cos[:, 0]
-        cos = sin_cos[:, 1]
+        position = build_positions(nc, keep)
+        frequency = build_frequencies(nc, keep)
+        first_steps, first_turns = angle_steps(nc, keep, position[:, 0:ROWS], frequency)
+        later_steps, later_turns = angle_steps(nc, keep, position[:, ROWS:SLOTS], frequency)
+        half_sines = keep.tile([P, 3, SLOTS, PAIRS], F32)
+        factors = keep.tile([P, 3, SLOTS, PAIRS], F32)
         identity = keep.tile([P, P], F32)
         make_identity(nc, identity[:])
+        for step in first_steps:
+            step()
+        build_factors(nc, factors, half_sines, first_turns[:], 0)
+        regroup_weight_block(Q_BLOCK, nc.vector.tensor_copy, nc.vector.tensor_copy)
         flip_chunk(0)
-        regroup_weight_block(Q_BLOCK, nc.vector.tensor_copy)
-        partner_factors = build_partner_factors(nc, keep, sin, cos)
         quantise_weight_block(Q_BLOCK)
         quantise_chunk(0)
-        regroup_weight_block(K_BLOCK, nc.scalar.copy)
-        regroup_weight_block(V_BLOCK, nc.scalar.copy)
         flip_chunk(1)
-        quantise_weight_block(K_BLOCK)
-        quantise_weight_block(V_BLOCK)
-        quantise_chunk(1)
+        regroup_weight_block(K_BLOCK, nc.vector.tensor_copy, nc.scalar.copy)
 
         def start_q(chunk):
-            q_rotated = results.tile([P, ROWS, BLOCK], F32)
-            q_sums = partner_products(chunk, Q_BLOCK, [q_rotated[:, row] for row in range(ROWS)])
-            return q_rotated, q_sums
+            rotated = results.tile([P, ROWS * BLOCK], F32)
+            return rotated, partner_products(rotated, chunk, Q_BLOCK)
 
         q_rotated, q_sums = start_q(0)
-        q_shared = shared_products(0, q_sums)
+        later_steps[0]()
+        quantise_weight_block(K_BLOCK)
+        later_steps[1]()
+        quantise_chunk(1)
+        later_steps[2]()
+        regroup_weight_block(V_BLOCK, nc.scalar.copy, nc.scalar.copy)
         for chunk in range(CHUNKS):
-            q_flat = q_rotated[:].rearrange("p r n -> p (r n)")
-            add_shared(nc.gpsimd, q_flat, q_flat, q_shared[:].rearrange("p r n -> p (r n)"))
-            store(out_0, chunk, q_rotated)
-            k_rotated = results.tile([P, ROWS, BLOCK], F32)
-            k_first = results.tile([P, BLOCK], F32)
-            k_sums = partner_products(chunk, K_BLOCK, [k_first[:], k_rotated[:, 0]])
-            k_shared = shared_products(chunk, k_sums)
-            project_values(chunk)
+            last_chunk = chunk + 1 == CHUNKS
+            q_shared = results.tile([P, ROWS * HALF], F32)
+            shared_products(q_shared[:], chunk, q_sums)
+            q_by_gpsimd = BLOCK if last_chunk else ROWS * BLOCK
+            add_shared(nc.gpsimd, q_rotated, q_rotated, q_shared, 0, q_by_gpsimd)
+            if not last_chunk:
+                store(out_0, chunk, q_rotated[:])
+
+            k_products = results.tile([P, ROWS * BLOCK], F32)
+            k_work = results.tile([P, ROWS * HALF - K_BY_GPSIMD + ROWS * BLOCK], F32)
+            k_shared = k_work[:, 0 : ROWS * HALF]
+            k_rotated = k_work[:, ROWS * HALF - K_BY_GPSIMD :]
+            k_sums = partner_products(k_products, chunk, K_BLOCK)
+            shared_products(k_shared, chunk, k_sums)
+            if chunk > 0:
+                project_values(chunk - 1)
+            if last_chunk:
+                project_values(chunk)
+                add_shared(nc.vector, q_rotated, q_rotated, q_shared, BLOCK, ROWS * BLOCK)
+                store(out_0, chunk, q_rotated[:])
+                add_shared(nc.vector, k_rotated, k_products, k_shared, BLOCK, ROWS * BLOCK)
+                store(out_1, chunk, k_rotated, 1, 2)
+                add_shared(nc.vector, k_rotated, k_products, k_shared, K_BY_GPSIMD, BLOCK)
+                add_shared(nc.vector, k_rotated, k_products, k_shared, 0, K_BY_GPSIMD)
+                store(out_1, chunk, k_rotated, 0, 1)
+                break
             if chunk + 2 < CHUNKS:
                 flip_chunk(chunk + 2)
-            if chunk + 1 < CHUNKS:
-                q_rotated, q_sums = start_q(chunk + 1)
+            if chunk + 1 < CHUNKS_PER_SEQ:
+                rows = slice(chunk * ROWS, (chunk + 1) * ROWS)
+                build_factors(nc, factors, half_sines, later_turns[:, rows], (chunk + 1) * ROWS)
+            q_rotated, q_sums = start_q(chunk + 1)
+            if chunk == 0:
+                quantise_weight_block(V_BLOCK)
             if chunk + 2 < CHUNKS:
                 quantise_chunk(chunk + 2)
-            add_shared(nc.vector, k_rotated[:, 1], k_rotated[:, 0], k_shared[:, 1])
-            add_shared(nc.gpsimd, k_rotated[:, 0], k_first[:], k_shared[:, 0])
+            add_shared(nc.vector, k_rotated, k_products, k_shared, K_BY_GPSIMD, ROWS * BLOCK)
+            add_shared(nc.gpsimd, k_rotated, k_products, k_shared, 0, K_BY_GPSIMD)
             store(out_1, chunk, k_rotated)
-            if chunk + 1 < CHUNKS:
-                q_shared = shared_products(chunk + 1, q_sums)

@@ -31,7 +31,9 @@ CHUNKS_PER_SEQ = SEQ // CHUNK
 CHUNKS = BATCH * CHUNKS_PER_SEQ
 SLOTS = CHUNKS_PER_SEQ * ROWS
 Q_BLOCK, K_BLOCK, V_BLOCK = 0, 1, 2
-K_BY_GPSIMD = 256
+ROTATED = 2 * ROWS * BLOCK
+BY_GPSIMD = ROWS * BLOCK + 256
+OVERLAP = 256
 ROUND = 12582912.0
 
 FLOPS = 2 * BATCH * SEQ * K * 3 * BLOCK
@@ -118,7 +120,7 @@ def tile_memoryselfattention_pa_t_kernel(
     with ExitStack() as ctx:
         keep = ctx.enter_context(tc.tile_pool(name="keep", bufs=1))
         stage = ctx.enter_context(tc.tile_pool(name="stage", bufs=4))
-        results = ctx.enter_context(tc.tile_pool(name="results", bufs=6))
+        results = ctx.enter_context(tc.tile_pool(name="results", bufs=4))
         flipped_banks = ctx.enter_context(tc.psum_pool(name="flipped_banks", bufs=2))
         sum_banks = ctx.enter_context(tc.psum_pool(name="sum_banks", bufs=2))
         product_banks = ctx.enter_context(tc.psum_pool(name="product_banks", bufs=4))
@@ -296,11 +298,18 @@ def tile_memoryselfattention_pa_t_kernel(
         flip_chunk(1)
         regroup_weight_block(K_BLOCK, nc.vector.tensor_copy, nc.scalar.copy)
 
-        def start_q(chunk):
-            rotated = results.tile([P, ROWS * BLOCK], F32)
-            return rotated, partner_products(rotated, chunk, Q_BLOCK)
+        def start_chunk():
+            products = results.tile([P, ROTATED], F32)
+            work = results.tile([P, ROTATED // 2 - OVERLAP + ROTATED], F32)
+            return products, work[:, 0 : ROTATED // 2], work[:, ROTATED // 2 - OVERLAP :]
 
-        q_rotated, q_sums = start_q(0)
+        def rotate(block, chunk, products, shared):
+            columns = slice(ROWS * BLOCK * block, ROWS * BLOCK * (block + 1))
+            sums = partner_products(products[:, columns], chunk, block)
+            shared_products(shared[:, columns.start // 2 : columns.stop // 2], chunk, sums)
+
+        products, shared, rotated = start_chunk()
+        rotate(Q_BLOCK, 0, products, shared)
         later_steps[0]()
         quantise_weight_block(K_BLOCK)
         later_steps[1]()
@@ -308,42 +317,31 @@ def tile_memoryselfattention_pa_t_kernel(
         later_steps[2]()
         regroup_weight_block(V_BLOCK, nc.scalar.copy, nc.scalar.copy)
         for chunk in range(CHUNKS):
-            last_chunk = chunk + 1 == CHUNKS
-            q_shared = results.tile([P, ROWS * HALF], F32)
-            shared_products(q_shared[:], chunk, q_sums)
-            q_by_gpsimd = BLOCK if last_chunk else ROWS * BLOCK
-            add_shared(nc.gpsimd, q_rotated, q_rotated, q_shared, 0, q_by_gpsimd)
-            if not last_chunk:
-                store(out_0, chunk, q_rotated[:])
-
-            k_products = results.tile([P, ROWS * BLOCK], F32)
-            k_work = results.tile([P, ROWS * HALF - K_BY_GPSIMD + ROWS * BLOCK], F32)
-            k_shared = k_work[:, 0 : ROWS * HALF]
-            k_rotated = k_work[:, ROWS * HALF - K_BY_GPSIMD :]
-            k_sums = partner_products(k_products, chunk, K_BLOCK)
-            shared_products(k_shared, chunk, k_sums)
+            rotate(K_BLOCK, chunk, products, shared)
             if chunk > 0:
                 project_values(chunk - 1)
-            if last_chunk:
-                project_values(chunk)
-                add_shared(nc.vector, q_rotated, q_rotated, q_shared, BLOCK, ROWS * BLOCK)
-                store(out_0, chunk, q_rotated[:])
-                add_shared(nc.vector, k_rotated, k_products, k_shared, BLOCK, ROWS * BLOCK)
-                store(out_1, chunk, k_rotated, 1, 2)
-                add_shared(nc.vector, k_rotated, k_products, k_shared, K_BY_GPSIMD, BLOCK)
-                add_shared(nc.vector, k_rotated, k_products, k_shared, 0, K_BY_GPSIMD)
-                store(out_1, chunk, k_rotated, 0, 1)
+            if chunk + 1 == CHUNKS:
                 break
             if chunk + 2 < CHUNKS:
                 flip_chunk(chunk + 2)
             if chunk + 1 < CHUNKS_PER_SEQ:
                 rows = slice(chunk * ROWS, (chunk + 1) * ROWS)
                 build_factors(nc, factors, half_sines, later_turns[:, rows], (chunk + 1) * ROWS)
-            q_rotated, q_sums = start_q(chunk + 1)
             if chunk == 0:
                 quantise_weight_block(V_BLOCK)
             if chunk + 2 < CHUNKS:
                 quantise_chunk(chunk + 2)
-            add_shared(nc.vector, k_rotated, k_products, k_shared, K_BY_GPSIMD, ROWS * BLOCK)
-            add_shared(nc.gpsimd, k_rotated, k_products, k_shared, 0, K_BY_GPSIMD)
-            store(out_1, chunk, k_rotated)
+            add_shared(nc.vector, rotated, products, shared, BY_GPSIMD, ROTATED)
+            add_shared(nc.gpsimd, rotated, products, shared, 0, BY_GPSIMD)
+            store(out_0, chunk, rotated[:, 0 : ROWS * BLOCK])
+            store(out_1, chunk, rotated[:, ROWS * BLOCK : ROTATED])
+            products, shared, rotated = start_chunk()
+            rotate(Q_BLOCK, chunk + 1, products, shared)
+
+        project_values(CHUNKS - 1)
+        for out, first in ((out_1, ROWS * BLOCK), (out_0, 0)):
+            tokens = rotated[:, first : first + ROWS * BLOCK]
+            for row in reversed(range(ROWS)):
+                start = first + BLOCK * row
+                add_shared(nc.vector, rotated, products, shared, start, start + BLOCK)
+                store(out, CHUNKS - 1, tokens, row, row + 1)

@@ -23,7 +23,8 @@ BLOCK = 512
 HALF = BLOCK // 2
 HEADS = 4
 PAIRS = 64
-DOUBLINGS = 6
+FOLD = 4
+FOLDS = 3
 THETA = 10000.0
 ROWS = 2
 CHUNK = P * ROWS
@@ -55,13 +56,14 @@ def build_positions(nc, pool):
 def build_frequencies(nc, pool):
     frequency = pool.tile([P, PAIRS], F32)
     nc.vector.memset(frequency[:, 0:1], 1.0)
-    for doubling in range(DOUBLINGS):
-        width = 2**doubling
-        nc.vector.tensor_scalar_mul(
-            out=frequency[:, width : 2 * width],
-            in0=frequency[:, 0:width],
-            scalar1=THETA ** (-width / PAIRS),
-        )
+    for fold in range(FOLDS):
+        width = FOLD**fold
+        for j in range(1, FOLD):
+            nc.vector.tensor_scalar_mul(
+                out=frequency[:, j * width : (j + 1) * width],
+                in0=frequency[:, 0:width],
+                scalar1=THETA ** (-j * width / PAIRS),
+            )
     return frequency
 
 
@@ -288,11 +290,12 @@ def tile_memoryselfattention_pa_t_kernel(
         factors = keep.tile([P, 3, SLOTS, PAIRS], F32)
         identity = keep.tile([P, P], F32)
         make_identity(nc, identity[:])
-        for step in first_steps:
-            step()
+        for first_step, later_step in zip(first_steps, later_steps):
+            first_step()
+            later_step()
         build_factors(nc, factors, half_sines, first_turns[:], 0)
-        regroup_weight_block(Q_BLOCK, nc.vector.tensor_copy, nc.vector.tensor_copy)
         flip_chunk(0)
+        regroup_weight_block(Q_BLOCK, nc.vector.tensor_copy, nc.vector.tensor_copy)
         quantise_weight_block(Q_BLOCK)
         quantise_chunk(0)
         flip_chunk(1)
@@ -310,20 +313,21 @@ def tile_memoryselfattention_pa_t_kernel(
 
         products, shared, rotated = start_chunk()
         rotate(Q_BLOCK, 0, products, shared)
-        later_steps[0]()
         quantise_weight_block(K_BLOCK)
-        later_steps[1]()
         quantise_chunk(1)
-        later_steps[2]()
+        flip_chunk(2)
         regroup_weight_block(V_BLOCK, nc.scalar.copy, nc.scalar.copy)
+        values_done = 0
         for chunk in range(CHUNKS):
             rotate(K_BLOCK, chunk, products, shared)
-            if chunk > 0:
-                project_values(chunk - 1)
             if chunk + 1 == CHUNKS:
                 break
-            if chunk + 2 < CHUNKS:
-                flip_chunk(chunk + 2)
+            if chunk + 3 < CHUNKS:
+                flip_chunk(chunk + 3)
+            values_due = min(2 * chunk, chunk + 2, CHUNKS)
+            for value_chunk in range(values_done, values_due):
+                project_values(value_chunk)
+            values_done = values_due
             if chunk + 1 < CHUNKS_PER_SEQ:
                 rows = slice(chunk * ROWS, (chunk + 1) * ROWS)
                 build_factors(nc, factors, half_sines, later_turns[:, rows], (chunk + 1) * ROWS)
@@ -332,13 +336,17 @@ def tile_memoryselfattention_pa_t_kernel(
             if chunk + 2 < CHUNKS:
                 quantise_chunk(chunk + 2)
             add_shared(nc.vector, rotated, products, shared, BY_GPSIMD, ROTATED)
-            add_shared(nc.gpsimd, rotated, products, shared, 0, BY_GPSIMD)
-            store(out_0, chunk, rotated[:, 0 : ROWS * BLOCK])
+            if chunk + 2 < CHUNKS:
+                add_shared(nc.gpsimd, rotated, products, shared, 0, BY_GPSIMD)
+                store(out_0, chunk, rotated[:, 0 : ROWS * BLOCK])
+            else:
+                add_shared(nc.gpsimd, rotated, products, shared, 0, ROWS * BLOCK)
+                store(out_0, chunk, rotated[:, 0 : ROWS * BLOCK])
+                add_shared(nc.gpsimd, rotated, products, shared, ROWS * BLOCK, BY_GPSIMD)
             store(out_1, chunk, rotated[:, ROWS * BLOCK : ROTATED])
             products, shared, rotated = start_chunk()
             rotate(Q_BLOCK, chunk + 1, products, shared)
 
-        project_values(CHUNKS - 1)
         for out, first in ((out_1, ROWS * BLOCK), (out_0, 0)):
             tokens = rotated[:, first : first + ROWS * BLOCK]
             for row in reversed(range(ROWS)):

@@ -33,7 +33,8 @@ CHUNKS = BATCH * CHUNKS_PER_SEQ
 SLOTS = CHUNKS_PER_SEQ * ROWS
 Q_BLOCK, K_BLOCK, V_BLOCK = 0, 1, 2
 ROTATED = 2 * ROWS * BLOCK
-BY_GPSIMD = ROWS * BLOCK + 256
+BY_GPSIMD = ROWS * BLOCK + 192
+BY_TENSOR = BY_GPSIMD + 128
 OVERLAP = 256
 ROUND = 12582912.0
 
@@ -186,7 +187,7 @@ def tile_memoryselfattention_pa_t_kernel(
 
         def flip_chunk(chunk):
             words = x_rows[chunk][:].bitcast(F32)
-            flipped = flipped_banks.tile([P, ROWS, 2, P], F32)
+            flipped = flipped_banks.tile([P, ROWS, 2, P], F32, name="flipped")
             for row in range(ROWS):
                 for u in range(2):
                     nc.tensor.transpose(
@@ -272,6 +273,21 @@ def tile_memoryselfattention_pa_t_kernel(
                 op=ALU.add,
             )
 
+        def add_on_tensor(out, products, shared, first, last):
+            bank = flipped_banks.tile([P, last - first], F32, name="flipped")
+            pairs = (last - first) // 2
+            nc.tensor.matmul(
+                bank[:], lhsT=identity[:], rhs=products[:, first:last], start=True, stop=False
+            )
+            nc.tensor.matmul(
+                bank[:].rearrange("p (n e) -> p n e", e=2),
+                lhsT=identity[:],
+                rhs=shared[:, first // 2 : last // 2].unsqueeze(2).to_broadcast([P, pairs, 2]),
+                start=False,
+                stop=True,
+            )
+            nc.scalar.copy(out=out[:, first:last], in_=bank[:])
+
         def project_values(chunk):
             values = results.tile([P, ROWS * BLOCK], F32)
             for row in range(ROWS):
@@ -335,7 +351,7 @@ def tile_memoryselfattention_pa_t_kernel(
                 quantise_weight_block(V_BLOCK)
             if chunk + 2 < CHUNKS:
                 quantise_chunk(chunk + 2)
-            add_shared(nc.vector, rotated, products, shared, BY_GPSIMD, ROTATED)
+            add_shared(nc.vector, rotated, products, shared, BY_TENSOR, ROTATED)
             if chunk + 2 < CHUNKS:
                 add_shared(nc.gpsimd, rotated, products, shared, 0, BY_GPSIMD)
                 store(out_0, chunk, rotated[:, 0 : ROWS * BLOCK])
@@ -343,9 +359,11 @@ def tile_memoryselfattention_pa_t_kernel(
                 add_shared(nc.gpsimd, rotated, products, shared, 0, ROWS * BLOCK)
                 store(out_0, chunk, rotated[:, 0 : ROWS * BLOCK])
                 add_shared(nc.gpsimd, rotated, products, shared, ROWS * BLOCK, BY_GPSIMD)
+            next_products, next_shared, next_rotated = start_chunk()
+            rotate(Q_BLOCK, chunk + 1, next_products, next_shared)
+            add_on_tensor(rotated, products, shared, BY_GPSIMD, BY_TENSOR)
             store(out_1, chunk, rotated[:, ROWS * BLOCK : ROTATED])
-            products, shared, rotated = start_chunk()
-            rotate(Q_BLOCK, chunk + 1, products, shared)
+            products, shared, rotated = next_products, next_shared, next_rotated
 
         for out, first in ((out_1, ROWS * BLOCK), (out_0, 0)):
             tokens = rotated[:, first : first + ROWS * BLOCK]

@@ -33,7 +33,7 @@ CHUNKS = BATCH * CHUNKS_PER_SEQ
 SLOTS = CHUNKS_PER_SEQ * ROWS
 Q_BLOCK, K_BLOCK, V_BLOCK = 0, 1, 2
 ROTATED = 2 * ROWS * BLOCK
-BY_GPSIMD = ROWS * BLOCK + 192
+BY_GPSIMD = ROWS * BLOCK + 320
 BY_TENSOR = BY_GPSIMD + 128
 OVERLAP = 256
 ROUND = 12582912.0
@@ -365,9 +365,13 @@ def tile_memoryselfattention_pa_t_kernel(
             store(out_1, chunk, rotated[:, ROWS * BLOCK : ROTATED])
             products, shared, rotated = next_products, next_shared, next_rotated
 
-        for out, first in ((out_1, ROWS * BLOCK), (out_0, 0)):
-            tokens = rotated[:, first : first + ROWS * BLOCK]
-            for row in reversed(range(ROWS)):
-                start = first + BLOCK * row
-                add_shared(nc.vector, rotated, products, shared, start, start + BLOCK)
-                store(out, CHUNKS - 1, tokens, row, row + 1)
+        q_tokens = rotated[:, 0 : ROWS * BLOCK]
+        k_tokens = rotated[:, ROWS * BLOCK : ROTATED]
+        for row in reversed(range(ROWS)):
+            start = ROWS * BLOCK + BLOCK * row
+            add_shared(nc.vector, rotated, products, shared, start, start + BLOCK)
+            store(out_1, CHUNKS - 1, k_tokens, row, row + 1)
+        add_on_tensor(rotated, products, shared, BLOCK, ROWS * BLOCK)
+        store(out_0, CHUNKS - 1, q_tokens, 1, ROWS)
+        add_shared(nc.vector, rotated, products, shared, 0, BLOCK)
+        store(out_0, CHUNKS - 1, q_tokens, 0, 1)

import math
from contextlib import ExitStack

import concourse.mybir as mybir
from concourse.masks import make_identity

F32 = mybir.dt.float32
BF16 = mybir.dt.bfloat16
I32 = mybir.dt.int32
U32 = mybir.dt.uint32
U8 = mybir.dt.uint8
FP8X4 = mybir.dt.float8_e4m3fn_x4
ALU = mybir.AluOpType
ACT = mybir.ActivationFunctionType

P = 128
PACK = 4
BATCH = 4
SEQ = 1024
K = 512
WORDS = K // 2
BLOCK = 512
HALF = BLOCK // 2
HEADS = 4
PAIRS = 64
FOLD = 4
FOLDS = 3
THETA = 10000.0
ROWS = 2
CHUNK = P * ROWS
CHUNKS_PER_SEQ = SEQ // CHUNK
CHUNKS = BATCH * CHUNKS_PER_SEQ
SLOTS = CHUNKS_PER_SEQ * ROWS
Q_BLOCK, K_BLOCK, V_BLOCK = 0, 1, 2
ROTATED = 2 * ROWS * BLOCK
BY_GPSIMD = ROWS * BLOCK + 320
BY_TENSOR = BY_GPSIMD + 128
OVERLAP = 256
ROUND = 12582912.0

FLOPS = 2 * BATCH * SEQ * K * 3 * BLOCK


def build_positions(nc, pool):
    position = pool.tile([P, SLOTS], I32)
    nc.gpsimd.iota(
        position[:],
        pattern=[[CHUNK, CHUNKS_PER_SEQ], [1, ROWS]],
        base=0,
        channel_multiplier=ROWS,
    )
    position_f32 = pool.tile([P, SLOTS], F32)
    nc.vector.tensor_copy(out=position_f32[:], in_=position[:])
    return position_f32


def build_frequencies(nc, pool):
    frequency = pool.tile([P, PAIRS], F32)
    nc.vector.memset(frequency[:, 0:1], 1.0)
    for fold in range(FOLDS):
        width = FOLD**fold
        for j in range(1, FOLD):
            nc.vector.tensor_scalar_mul(
                out=frequency[:, j * width : (j + 1) * width],
                in0=frequency[:, 0:width],
                scalar1=THETA ** (-j * width / PAIRS),
            )
    return frequency


def angle_steps(nc, pool, position, frequency):
    slots = position.shape[1]
    turns = pool.tile([P, slots, PAIRS], F32, name="turns%d" % slots)
    whole = pool.tile([P, slots, PAIRS], F32, name="whole%d" % slots)
    fraction = pool.tile([P, slots, PAIRS], F32, name="fraction%d" % slots)

    def multiply_out():
        nc.vector.scalar_tensor_tensor(
            out=turns[:],
            in0=position.unsqueeze(2).to_broadcast([P, slots, PAIRS]),
            scalar=1.0 / (2.0 * math.pi),
            in1=frequency[:].unsqueeze(1).to_broadcast([P, slots, PAIRS]),
            op0=ALU.mult,
            op1=ALU.mult,
        )

    def round_off():
        nc.vector.tensor_scalar(
            out=whole[:], in0=turns[:], scalar1=ROUND, scalar2=ROUND, op0=ALU.add, op1=ALU.subtract
        )

    def take_away():
        nc.vector.tensor_tensor(out=fraction[:], in0=turns[:], in1=whole[:], op=ALU.subtract)

    return (multiply_out, round_off, take_away), fraction


def build_factors(nc, factors, half_sines, turns, first_slot):
    slots = slice(first_slot, first_slot + ROWS)
    for plane, shift in enumerate((-0.125, 0.125, 0.0)):
        nc.scalar.activation(
            out=half_sines[:, plane, slots],
            in_=turns,
            func=ACT.Sin,
            scale=math.pi,
            bias=shift * math.pi,
        )
    nc.scalar.square(half_sines[:, :, slots], half_sines[:, :, slots])
    for first, last, size in ((0, 2, -math.sqrt(2.0)), (2, 3, 1.0)):
        nc.scalar.activation(
            out=factors[:, first:last, slots],
            in_=half_sines[:, first:last, slots],
            func=ACT.Copy,
            scale=-2.0 * size,
            bias=size,
        )


def tile_memoryselfattention_pa_t_kernel(
    tc, x, short_term_memory, w_attn, out_0, out_1, out_2
):
    nc = tc.nc
    with ExitStack() as ctx:
        keep = ctx.enter_context(tc.tile_pool(name="keep", bufs=1))
        stage = ctx.enter_context(tc.tile_pool(name="stage", bufs=4))
        results = ctx.enter_context(tc.tile_pool(name="results", bufs=4))
        flipped_banks = ctx.enter_context(tc.psum_pool(name="flipped_banks", bufs=2))
        sum_banks = ctx.enter_context(tc.psum_pool(name="sum_banks", bufs=2))
        product_banks = ctx.enter_context(tc.psum_pool(name="product_banks", bufs=4))
        ctx.enter_context(tc.manual_schedule())

        x_rows = [
            keep.tile([P, ROWS, K], BF16, name="x_rows%d" % chunk) for chunk in range(CHUNKS)
        ]
        w_rows = keep.tile([P, 3, PACK, BLOCK], BF16)

        def load_chunk(chunk):
            part, batch = divmod(chunk, BATCH)
            if part == 0:
                rows = short_term_memory[batch]
            else:
                rows = x[batch, (part - 1) * CHUNK : part * CHUNK]
            nc.sync.dma_start(
                out=x_rows[chunk][:], in_=rows.rearrange("(p r) k -> p r k", r=ROWS)
            )

        def load_weight_block(block):
            for u in range(2):
                nc.sync.dma_start(
                    out=w_rows[:, block, 2 * u : 2 * u + 2, :],
                    in_=w_attn[
                        WORDS * u : WORDS * (u + 1), BLOCK * block : BLOCK * (block + 1)
                    ].rearrange("(p e) c -> p e c", e=2),
                )

        load_weight_block(Q_BLOCK)
        load_chunk(0)
        load_chunk(1)
        load_weight_block(K_BLOCK)
        load_weight_block(V_BLOCK)
        for chunk in range(2, CHUNKS):
            load_chunk(chunk)

        w_grouped = keep.tile([P, 3, 2, HALF, PACK], BF16, align_bytes=64)
        w_codes = keep.tile([P, 3, BLOCK], U32, align_bytes=64)
        w_scales = keep.tile([P, 3, BLOCK], U8, align_bytes=64)

        def regroup_weight_block(block, copy_first_half, copy_second_half):
            if block == V_BLOCK:
                halves = w_rows[:, block].rearrange("p t (g n) -> p g n t", g=2)
                first, second = halves[:, 0], halves[:, 1]
            else:
                parities = w_rows[:, block].rearrange("p t (n e) -> p e n t", e=2)
                first, second = parities[:, 1], parities[:, 0]
            copy_first_half(out=w_grouped[:, block, 0], in_=first)
            copy_second_half(out=w_grouped[:, block, 1], in_=second)

        def quantise_weight_block(block):
            nc.vector.quantize_mx(
                out=w_codes[:, block, :].bitcast(FP8X4),
                scales=w_scales[:, block, :],
                in_=w_grouped[:, block].rearrange("p g n t -> p (g n t)"),
            )

        x_grouped = {}
        x_operands = {}

        def flip_chunk(chunk):
            words = x_rows[chunk][:].bitcast(F32)
            flipped = flipped_banks.tile([P, ROWS, 2, P], F32, name="flipped")
            for row in range(ROWS):
                for u in range(2):
                    nc.tensor.transpose(
                        flipped[:, row, u, :], words[:, row, P * u : P * (u + 1)], identity[:]
                    )
            grouped = stage.tile([P, ROWS * P * PACK], BF16, align_bytes=64)
            nc.scalar.copy(
                out=grouped[:].bitcast(F32).rearrange("p (r m u) -> p r m u", r=ROWS, u=2),
                in_=flipped[:].rearrange("p r u m -> p r m u"),
            )
            x_grouped[chunk] = grouped

        def quantise_chunk(chunk):
            codes = stage.tile([P, ROWS * P], U32, align_bytes=64)
            scales = stage.tile([P, ROWS * P], U8, align_bytes=64)
            nc.vector.quantize_mx(
                out=codes[:].bitcast(FP8X4), scales=scales[:], in_=x_grouped[chunk][:]
            )
            x_operands[chunk] = (codes, scales)

        def multiply(out, chunk, row, block, first, last, start, stop):
            codes, scales = x_operands[chunk]
            tokens = slice(P * row, P * (row + 1))
            nc.tensor.matmul_mx(
                out=out,
                lhsT=codes[:, tokens].bitcast(FP8X4),
                lhsT_scale=scales[:, tokens],
                rhs=w_codes[:, block, first:last].bitcast(FP8X4),
                rhs_scale=w_scales[:, block, first:last],
                start=start,
                stop=stop,
            )

        def store(out, chunk, tokens, first_row=0, last_row=ROWS):
            part, batch = divmod(chunk, BATCH)
            rows = slice(first_row, last_row)
            nc.sync.dma_start(
                out=out[batch, part * CHUNK : (part + 1) * CHUNK].rearrange(
                    "(p r) h d -> p r (h d)", r=ROWS
                )[:, rows],
                in_=tokens.rearrange("p (r n) -> p r n", r=ROWS)[:, rows],
            )

        def partner_products(out, chunk, block):
            part = chunk // BATCH
            pair_sums = sum_banks.tile([P, ROWS, HALF], F32)
            for row in range(ROWS):
                products = product_banks.tile([P, BLOCK], F32)
                multiply(products[:], chunk, row, block, 0, BLOCK, True, True)
                multiply(pair_sums[:, row], chunk, row, block, 0, HALF, True, False)
                multiply(pair_sums[:, row], chunk, row, block, HALF, BLOCK, False, True)
                nc.vector.tensor_tensor(
                    out=out[:, BLOCK * row : BLOCK * (row + 1)].rearrange(
                        "p (h i e) -> p h i e", h=HEADS, e=2
                    ),
                    in0=products[:].rearrange("p (e h i) -> p h i e", e=2, h=HEADS),
                    in1=factors[:, 0:2, part * ROWS + row, :]
                    .rearrange("p e i -> p i e")
                    .unsqueeze(1)
                    .to_broadcast([P, HEADS, PAIRS, 2]),
                    op=ALU.mult,
                )
            return pair_sums

        def shared_products(out, chunk, pair_sums):
            part = chunk // BATCH
            nc.vector.tensor_tensor(
                out=out.rearrange("p (r h i) -> p r h i", r=ROWS, h=HEADS),
                in0=pair_sums[:].rearrange("p r (h i) -> p r h i", h=HEADS),
                in1=factors[:, 2, part * ROWS : (part + 1) * ROWS, :]
                .unsqueeze(2)
                .to_broadcast([P, ROWS, HEADS, PAIRS]),
                op=ALU.mult,
            )

        def add_shared(engine, out, products, shared, first, last):
            engine.tensor_tensor(
                out=out[:, first:last].rearrange("p (n e) -> p n e", e=2),
                in0=products[:, first:last].rearrange("p (n e) -> p n e", e=2),
                in1=shared[:, first // 2 : last // 2]
                .unsqueeze(2)
                .to_broadcast([P, (last - first) // 2, 2]),
                op=ALU.add,
            )

        def add_on_tensor(out, products, shared, first, last):
            bank = flipped_banks.tile([P, last - first], F32, name="flipped")
            pairs = (last - first) // 2
            nc.tensor.matmul(
                bank[:], lhsT=identity[:], rhs=products[:, first:last], start=True, stop=False
            )
            nc.tensor.matmul(
                bank[:].rearrange("p (n e) -> p n e", e=2),
                lhsT=identity[:],
                rhs=shared[:, first // 2 : last // 2].unsqueeze(2).to_broadcast([P, pairs, 2]),
                start=False,
                stop=True,
            )
            nc.scalar.copy(out=out[:, first:last], in_=bank[:])

        def project_values(chunk):
            values = results.tile([P, ROWS * BLOCK], F32)
            for row in range(ROWS):
                products = product_banks.tile([P, BLOCK], F32)
                multiply(products[:], chunk, row, V_BLOCK, 0, BLOCK, True, True)
                nc.scalar.copy(
                    out=values[:, BLOCK * row : BLOCK * (row + 1)], in_=products[:]
                )
            store(out_2, chunk, values[:])

        position = build_positions(nc, keep)
        frequency = build_frequencies(nc, keep)
        first_steps, first_turns = angle_steps(nc, keep, position[:, 0:ROWS], frequency)
        later_steps, later_turns = angle_steps(nc, keep, position[:, ROWS:SLOTS], frequency)
        half_sines = keep.tile([P, 3, SLOTS, PAIRS], F32)
        factors = keep.tile([P, 3, SLOTS, PAIRS], F32)
        identity = keep.tile([P, P], F32)
        make_identity(nc, identity[:])
        for first_step, later_step in zip(first_steps, later_steps):
            first_step()
            later_step()
        build_factors(nc, factors, half_sines, first_turns[:], 0)
        flip_chunk(0)
        regroup_weight_block(Q_BLOCK, nc.vector.tensor_copy, nc.vector.tensor_copy)
        quantise_weight_block(Q_BLOCK)
        quantise_chunk(0)
        flip_chunk(1)
        regroup_weight_block(K_BLOCK, nc.vector.tensor_copy, nc.scalar.copy)

        def start_chunk():
            products = results.tile([P, ROTATED], F32)
            work = results.tile([P, ROTATED // 2 - OVERLAP + ROTATED], F32)
            return products, work[:, 0 : ROTATED // 2], work[:, ROTATED // 2 - OVERLAP :]

        def rotate(block, chunk, products, shared):
            columns = slice(ROWS * BLOCK * block, ROWS * BLOCK * (block + 1))
            sums = partner_products(products[:, columns], chunk, block)
            shared_products(shared[:, columns.start // 2 : columns.stop // 2], chunk, sums)

        products, shared, rotated = start_chunk()
        rotate(Q_BLOCK, 0, products, shared)
        quantise_weight_block(K_BLOCK)
        quantise_chunk(1)
        flip_chunk(2)
        regroup_weight_block(V_BLOCK, nc.scalar.copy, nc.scalar.copy)
        values_done = 0
        for chunk in range(CHUNKS):
            rotate(K_BLOCK, chunk, products, shared)
            if chunk + 1 == CHUNKS:
                break
            if chunk + 3 < CHUNKS:
                flip_chunk(chunk + 3)
            values_due = min(2 * chunk, chunk + 2, CHUNKS)
            for value_chunk in range(values_done, values_due):
                project_values(value_chunk)
            values_done = values_due
            if chunk + 1 < CHUNKS_PER_SEQ:
                rows = slice(chunk * ROWS, (chunk + 1) * ROWS)
                build_factors(nc, factors, half_sines, later_turns[:, rows], (chunk + 1) * ROWS)
            if chunk == 0:
                quantise_weight_block(V_BLOCK)
            if chunk + 2 < CHUNKS:
                quantise_chunk(chunk + 2)
            add_shared(nc.vector, rotated, products, shared, BY_TENSOR, ROTATED)
            if chunk + 2 < CHUNKS:
                add_shared(nc.gpsimd, rotated, products, shared, 0, BY_GPSIMD)
                store(out_0, chunk, rotated[:, 0 : ROWS * BLOCK])
            else:
                add_shared(nc.gpsimd, rotated, products, shared, 0, ROWS * BLOCK)
                store(out_0, chunk, rotated[:, 0 : ROWS * BLOCK])
                add_shared(nc.gpsimd, rotated, products, shared, ROWS * BLOCK, BY_GPSIMD)
            next_products, next_shared, next_rotated = start_chunk()
            rotate(Q_BLOCK, chunk + 1, next_products, next_shared)
            add_on_tensor(rotated, products, shared, BY_GPSIMD, BY_TENSOR)
            store(out_1, chunk, rotated[:, ROWS * BLOCK : ROTATED])
            products, shared, rotated = next_products, next_shared, next_rotated

        q_tokens = rotated[:, 0 : ROWS * BLOCK]
        k_tokens = rotated[:, ROWS * BLOCK : ROTATED]
        for row in reversed(range(ROWS)):
            start = ROWS * BLOCK + BLOCK * row
            add_shared(nc.vector, rotated, products, shared, start, start + BLOCK)
            store(out_1, CHUNKS - 1, k_tokens, row, row + 1)
        add_on_tensor(rotated, products, shared, BLOCK, ROWS * BLOCK)
        store(out_0, CHUNKS - 1, q_tokens, 1, ROWS)
        add_shared(nc.vector, rotated, products, shared, 0, BLOCK)
        store(out_0, CHUNKS - 1, q_tokens, 0, 1)
